import numpy as np
import ml_dtypes


def mxq(x, axis, fmt="e4m3"):
    dtype, down = {"e4m3": (ml_dtypes.float8_e4m3fn, 7), "e5m2": (ml_dtypes.float8_e5m2, 14)}[fmt]
    v = np.moveaxis(np.asarray(x, np.float32).astype(ml_dtypes.bfloat16).astype(np.float64), axis, -1)
    blocks = v.reshape(v.shape[:-1] + (-1, 32))
    amax = np.abs(blocks).max(-1, keepdims=True)
    byte = np.maximum(np.where(amax > 0, np.frexp(amax)[1] - 1 + 127, 0) - down, 1)
    scale = np.exp2(byte - 127.0)
    codes = (blocks / scale).astype(np.float32).astype(dtype).astype(np.float64)
    return np.moveaxis((codes * scale).reshape(v.shape), -1, axis)


WIDE = False


def mx_kscale(k):
    if not WIDE:
        return np.ones(k)
    levels = np.array([10, -10, 5, -5, 0])
    a = np.random.permutation(np.resize(levels, k // 512 * 4)).reshape(k // 512, 4)
    idx = np.arange(k)
    return np.exp2(a[idx // 512, idx % 128 // 32])


BF16 = ml_dtypes.bfloat16


def bf(x):
    return np.asarray(x, np.float32).astype(BF16)


def f64(x):
    return np.asarray(x).astype(np.float64)


B, S, D, N, A, F = 64, 64, 512, 128, 128, 512


def setup_inputs():
    s, t, u = mx_kscale(D), mx_kscale(F), mx_kscale(F)
    return {
        "slots": bf(np.random.standard_normal((B, S, D)) * s),
        "ident": bf(np.random.standard_normal((N, F)) * t),
        "Wq": bf(np.random.standard_normal((F, D)) / np.sqrt(D) / s[None, :] * u[:, None]),
        "Wk": bf(np.random.standard_normal((F, F)) * 2.0 / np.sqrt(F) / t[None, :] / u[:, None]),
    }


def reference(slots, ident, Wq, Wk):
    q = mxq(f64(slots), 2, "e4m3") @ mxq(f64(Wq), 1, "e4m3").T
    k = mxq(f64(ident), 1, "e4m3") @ mxq(f64(Wk), 1, "e4m3").T
    logits = D ** (-0.5) * (mxq(k, 1, "e4m3") @ mxq(q, 2, "e4m3").transpose(0, 2, 1))
    e = np.exp(logits - logits.max(-1, keepdims=True))
    return e / e.sum(-1, keepdims=True)

@@ -1,0 +1,249 @@
+from contextlib import ExitStack
+
+import concourse.masks as masks
+import concourse.mybir as mybir
+
+F32 = mybir.dt.float32
+BF16 = mybir.dt.bfloat16
+U32 = mybir.dt.uint32
+U8 = mybir.dt.uint8
+FP8X4 = mybir.dt.float8_e4m3fn_x4
+
+P = 128
+PACK = 4
+FEATURES = P * PACK
+WORDS = FEATURES // 2
+BANK = 512
+
+SAMPLES = 64
+SLOTS = 64
+OBJECTS = 128
+SLAB = BANK
+SLAB_SAMPLES = SLAB // SLOTS
+N_SLABS = SAMPLES * SLOTS // SLAB
+SLAB_TILES = SLAB // P
+LOGIT_SCALE = FEATURES**-0.5
+
+FLOPS = 2 * FEATURES * FEATURES * (SAMPLES * SLOTS + OBJECTS) + 2 * SAMPLES * OBJECTS * SLOTS * FEATURES
+
+
+def tile_actionbindingattention_pb_kernel(tc, slots, ident, Wq, Wk, out):
+    nc = tc.nc
+    tokens = slots.flatten_outer_dims()
+
+    with ExitStack() as ctx:
+        resident = ctx.enter_context(tc.tile_pool(name="resident", bufs=1))
+        stream = ctx.enter_context(tc.tile_pool(name="stream", bufs=3))
+        slots_psum = ctx.enter_context(tc.psum_pool(name="slots_psum", bufs=2))
+        q_psum = ctx.enter_context(tc.psum_pool(name="q_psum", bufs=4))
+        logits_psum = ctx.enter_context(tc.psum_pool(name="logits_psum", bufs=2))
+        ctx.enter_context(tc.manual_schedule())
+
+        def transpose_rows(rows_sb, n_tiles, pool):
+            words = rows_sb[:].bitcast(F32)
+            banks = []
+            for first in range(0, n_tiles, 2):
+                tiles_here = min(2, n_tiles - first)
+                bank = pool.tile([P, BANK], F32, name="bank")
+                squares = bank[:].rearrange("w (u row) -> w u row", u=2)
+                for r in range(tiles_here):
+                    for u in range(2):
+                        start = (first + r) * WORDS + u * P
+                        nc.tensor.transpose(
+                            out=squares[:, u, r * P : (r + 1) * P],
+                            in_=words[:, start : start + P],
+                            identity=identity[:],
+                        )
+                banks.append((squares, first, tiles_here))
+            return banks
+
+        def regroup(banks, grouped, copy):
+            pairs = grouped[:].bitcast(F32)
+            for squares, first, tiles_here in banks:
+                copy(
+                    out=pairs[:, first * 2 * P : (first + tiles_here) * 2 * P].rearrange(
+                        "w (row u) -> w row u", u=2
+                    ),
+                    in_=squares[:, :, 0 : tiles_here * P].rearrange("w u row -> w row u"),
+                )
+
+        def quantise(grouped, pool, name):
+            n_columns = grouped.shape[1] // PACK
+            codes = pool.tile([P, n_columns], U32, name=name + "_codes", align_bytes=64)
+            scales = pool.tile([P, n_columns], U8, name=name + "_scales", align_bytes=64)
+            nc.vector.quantize_mx(out=codes[:].bitcast(FP8X4), scales=scales[:], in_=grouped[:])
+            return codes, scales
+
+        def project(weights, rows, row_tile, grouped, copy):
+            w_codes, w_scales = weights
+            r_codes, r_scales = rows
+            row_columns = slice(row_tile * P, (row_tile + 1) * P)
+            bank = q_psum.tile([P, BANK], F32, name="bank")
+            for t in range(PACK):
+                feature_columns = slice(t * P, (t + 1) * P)
+                nc.tensor.matmul_mx(
+                    out=bank[:, feature_columns],
+                    lhsT=w_codes[:, feature_columns].bitcast(FP8X4),
+                    lhsT_scale=w_scales[:, feature_columns],
+                    rhs=r_codes[:, row_columns].bitcast(FP8X4),
+                    rhs_scale=r_scales[:, row_columns],
+                    start=True,
+                    stop=True,
+                )
+            copy(
+                out=grouped[:, row_tile * BANK : (row_tile + 1) * BANK].rearrange(
+                    "p (row t) -> p row t", t=PACK
+                ),
+                in_=bank[:].rearrange("p (t row) -> p row t", t=PACK),
+            )
+
+        def load_rows(rows, n_tiles, pattern, name):
+            rows_sb = resident.tile([P, n_tiles * FEATURES], BF16, name=name)
+            nc.sync.dma_start(
+                out=rows_sb[:].rearrange("p (r d) -> p r d", r=n_tiles),
+                in_=rows.rearrange(pattern, p=P),
+            )
+            return rows_sb
+
+        wq_sb = load_rows(Wq, SLAB_TILES, "(p r) d -> p r d", "wq_sb")
+        slots_sb = [load_rows(tokens[0:SLAB, :], SLAB_TILES, "(r p) d -> p r d", "slots_sb0")]
+        wk_sb = load_rows(Wk, SLAB_TILES, "(p r) d -> p r d", "wk_sb")
+        ident_sb = load_rows(ident, 1, "(r p) d -> p r d", "ident_sb")
+        for i in range(1, N_SLABS):
+            slots_sb.append(
+                load_rows(tokens[i * SLAB : (i + 1) * SLAB, :], SLAB_TILES, "(r p) d -> p r d", "slots_sb%d" % i)
+            )
+
+        identity = resident.tile([P, P], F32, name="identity")
+        masks.make_identity(nc, identity[:])
+
+        warm = resident.tile([P, 1], F32, name="warm")
+        nc.vector.memset(warm[:], 0.0)
+        nc.scalar.activation(out=warm[:], in_=warm[:], func=mybir.ActivationFunctionType.Exp)
+
+        slots_banks = {}
+        slots_grouped = {}
+        slots_mx = {}
+        q_grouped = {}
+        q_mx = {}
+        logits = {}
+        shift = {}
+        probs = {}
+        sums = {}
+
+        def transpose_slab(i):
+            slots_banks[i] = transpose_rows(slots_sb[i], SLAB_TILES, slots_psum)
+
+        def regroup_slab(i):
+            slots_grouped[i] = stream.tile([P, SLAB * PACK], BF16, name="slots_grouped", align_bytes=64)
+            regroup(slots_banks[i], slots_grouped[i], nc.vector.tensor_copy)
+
+        def quantise_slab(i):
+            slots_mx[i] = quantise(slots_grouped[i], stream, "slots")
+
+        def project_slab(i):
+            q_grouped[i] = stream.tile([P, SLAB * PACK], BF16, name="q_grouped", align_bytes=64)
+            for row_tile in range(SLAB_TILES):
+                project(wq_mx, slots_mx[i], row_tile, q_grouped[i], nc.scalar.copy)
+
+        def quantise_q(i):
+            q_mx[i] = quantise(q_grouped[i], stream, "q")
+
+        def score(i):
+            logits[i] = logits_psum.tile([P, BANK], F32, name="logits")
+            nc.tensor.matmul_mx(
+                out=logits[i][:],
+                lhsT=k_mx[0][:].bitcast(FP8X4),
+                lhsT_scale=k_mx[1][:],
+                rhs=q_mx[i][0][:].bitcast(FP8X4),
+                rhs_scale=q_mx[i][1][:],
+                start=True,
+                stop=True,
+            )
+
+        def row_max(i):
+            top = stream.tile([P, SLAB_SAMPLES], F32, name="top")
+            nc.vector.tensor_reduce(
+                out=top[:],
+                in_=logits[i][:].rearrange("n (b s) -> n b s", s=SLOTS),
+                axis=mybir.AxisListType.X,
+                op=mybir.AluOpType.max,
+            )
+            shift[i] = stream.tile([P, SLAB_SAMPLES], F32, name="shift")
+            nc.vector.tensor_scalar_mul(out=shift[i][:], in0=top[:], scalar1=-LOGIT_SCALE)
+
+        def exponentials(i):
+            probs[i] = stream.tile([P, SLAB_SAMPLES, SLOTS], F32, name="probs")
+            sums[i] = stream.tile([P, SLAB_SAMPLES], F32, name="sums")
+            for b in range(SLAB_SAMPLES):
+                nc.scalar.activation(
+                    out=probs[i][:, b, :],
+                    in_=logits[i][:, b * SLOTS : (b + 1) * SLOTS],
+                    func=mybir.ActivationFunctionType.Exp,
+                    bias=shift[i][:, b : b + 1],
+                    scale=LOGIT_SCALE,
+                    accum_out=sums[i][:, b : b + 1],
+                )
+
+        def normalise_and_store(i):
+            inverse = stream.tile([P, SLAB_SAMPLES], F32, name="inverse")
+            nc.vector.reciprocal(out=inverse[:], in_=sums[i][:])
+            nc.vector.tensor_tensor(
+                out=probs[i][:],
+                in0=probs[i][:],
+                in1=inverse[:].unsqueeze(2).to_broadcast([P, SLAB_SAMPLES, SLOTS]),
+                op=mybir.AluOpType.mult,
+            )
+            nc.sync.dma_start(
+                out=out[i * SLAB_SAMPLES : (i + 1) * SLAB_SAMPLES].rearrange("b n s -> n b s"),
+                in_=probs[i][:],
+            )
+
+        def pipeline_step(s):
+            if s < N_SLABS:
+                quantise_q(s)
+                score(s)
+            if s + 3 < N_SLABS:
+                regroup_slab(s + 3)
+            if s + 4 < N_SLABS:
+                transpose_slab(s + 4)
+            if s < N_SLABS:
+                row_max(s)
+                exponentials(s)
+            if s + 2 < N_SLABS:
+                project_slab(s + 2)
+            if s + 3 < N_SLABS:
+                quantise_slab(s + 3)
+            if s >= 1:
+                normalise_and_store(s - 1)
+
+        wq_grouped = resident.tile([P, FEATURES * PACK], BF16, name="wq_grouped", align_bytes=64)
+        regroup(transpose_rows(wq_sb, SLAB_TILES, q_psum), wq_grouped, nc.scalar.copy)
+        transpose_slab(0)
+        regroup_slab(0)
+        wq_mx = quantise(wq_grouped, resident, "wq")
+        quantise_slab(0)
+
+        wk_grouped = resident.tile([P, FEATURES * PACK], BF16, name="wk_grouped", align_bytes=64)
+        regroup(transpose_rows(wk_sb, SLAB_TILES, q_psum), wk_grouped, nc.scalar.copy)
+        ident_grouped = resident.tile([P, OBJECTS * PACK], BF16, name="ident_grouped", align_bytes=64)
+        regroup(transpose_rows(ident_sb, 1, q_psum), ident_grouped, nc.scalar.copy)
+
+        transpose_slab(1)
+        project_slab(0)
+        regroup_slab(1)
+        wk_mx = quantise(wk_grouped, resident, "wk")
+        ident_mx = quantise(ident_grouped, resident, "ident")
+        quantise_slab(1)
+
+        transpose_slab(2)
+        regroup_slab(2)
+        k_grouped = resident.tile([P, OBJECTS * PACK], BF16, name="k_grouped", align_bytes=64)
+        project(wk_mx, ident_mx, 0, k_grouped, nc.scalar.copy)
+        project_slab(1)
+        k_mx = quantise(k_grouped, resident, "k")
+        quantise_slab(2)
+        transpose_slab(3)
+
+        for s in range(N_SLABS + 1):
+            pipeline_step(s)

@@ -37,7 +37,6 @@ def tile_actionbindingattention_pb_kernel(tc, slots, ident, Wq, Wk, out):
         slots_psum = ctx.enter_context(tc.psum_pool(name="slots_psum", bufs=2))
         q_psum = ctx.enter_context(tc.psum_pool(name="q_psum", bufs=4))
         logits_psum = ctx.enter_context(tc.psum_pool(name="logits_psum", bufs=2))
-        ctx.enter_context(tc.manual_schedule())
 
         def transpose_rows(rows_sb, n_tiles, pool):
             words = rows_sb[:].bitcast(F32)
@@ -57,9 +56,9 @@ def tile_actionbindingattention_pb_kernel(tc, slots, ident, Wq, Wk, out):
                 banks.append((squares, first, tiles_here))
             return banks
 
-        def regroup(banks, grouped, copy):
+        def regroup(banks, grouped, copies):
             pairs = grouped[:].bitcast(F32)
-            for squares, first, tiles_here in banks:
+            for (squares, first, tiles_here), copy in zip(banks, copies):
                 copy(
                     out=pairs[:, first * 2 * P : (first + tiles_here) * 2 * P].rearrange(
                         "w (row u) -> w row u", u=2
@@ -136,7 +135,7 @@ def tile_actionbindingattention_pb_kernel(tc, slots, ident, Wq, Wk, out):
 
         def regroup_slab(i):
             slots_grouped[i] = stream.tile([P, SLAB * PACK], BF16, name="slots_grouped", align_bytes=64)
-            regroup(slots_banks[i], slots_grouped[i], nc.vector.tensor_copy)
+            regroup(slots_banks[i], slots_grouped[i], [nc.vector.tensor_copy, nc.scalar.copy])
 
         def quantise_slab(i):
             slots_mx[i] = quantise(slots_grouped[i], stream, "slots")
@@ -144,7 +143,7 @@ def tile_actionbindingattention_pb_kernel(tc, slots, ident, Wq, Wk, out):
         def project_slab(i):
             q_grouped[i] = stream.tile([P, SLAB * PACK], BF16, name="q_grouped", align_bytes=64)
             for row_tile in range(SLAB_TILES):
-                project(wq_mx, slots_mx[i], row_tile, q_grouped[i], nc.scalar.copy)
+                project(wq_mx, slots_mx[i], row_tile, q_grouped[i], nc.any.tensor_copy)
 
         def quantise_q(i):
             q_mx[i] = quantise(q_grouped[i], stream, "q")
@@ -218,16 +217,16 @@ def tile_actionbindingattention_pb_kernel(tc, slots, ident, Wq, Wk, out):
                 normalise_and_store(s - 1)
 
         wq_grouped = resident.tile([P, FEATURES * PACK], BF16, name="wq_grouped", align_bytes=64)
-        regroup(transpose_rows(wq_sb, SLAB_TILES, q_psum), wq_grouped, nc.scalar.copy)
+        regroup(transpose_rows(wq_sb, SLAB_TILES, q_psum), wq_grouped, [nc.scalar.copy, nc.scalar.copy])
         transpose_slab(0)
         regroup_slab(0)
         wq_mx = quantise(wq_grouped, resident, "wq")
         quantise_slab(0)
 
         wk_grouped = resident.tile([P, FEATURES * PACK], BF16, name="wk_grouped", align_bytes=64)
-        regroup(transpose_rows(wk_sb, SLAB_TILES, q_psum), wk_grouped, nc.scalar.copy)
+        regroup(transpose_rows(wk_sb, SLAB_TILES, q_psum), wk_grouped, [nc.scalar.copy, nc.scalar.copy])
         ident_grouped = resident.tile([P, OBJECTS * PACK], BF16, name="ident_grouped", align_bytes=64)
-        regroup(transpose_rows(ident_sb, 1, q_psum), ident_grouped, nc.scalar.copy)
+        regroup(transpose_rows(ident_sb, 1, q_psum), ident_grouped, [nc.scalar.copy])
 
         transpose_slab(1)
         project_slab(0)

@@ -14,14 +14,14 @@ PACK = 4
 FEATURES = P * PACK
 WORDS = FEATURES // 2
 BANK = 512
+PAIR = 2 * P
 
 SAMPLES = 64
 SLOTS = 64
 OBJECTS = 128
-SLAB = BANK
+SLAB = 256
 SLAB_SAMPLES = SLAB // SLOTS
 N_SLABS = SAMPLES * SLOTS // SLAB
-SLAB_TILES = SLAB // P
 LOGIT_SCALE = FEATURES**-0.5
 
 FLOPS = 2 * FEATURES * FEATURES * (SAMPLES * SLOTS + OBJECTS) + 2 * SAMPLES * OBJECTS * SLOTS * FEATURES
@@ -33,38 +33,37 @@ def tile_actionbindingattention_pb_kernel(tc, slots, ident, Wq, Wk, out):
 
     with ExitStack() as ctx:
         resident = ctx.enter_context(tc.tile_pool(name="resident", bufs=1))
-        stream = ctx.enter_context(tc.tile_pool(name="stream", bufs=3))
+        stream = ctx.enter_context(tc.tile_pool(name="stream", bufs=4))
         slots_psum = ctx.enter_context(tc.psum_pool(name="slots_psum", bufs=2))
         q_psum = ctx.enter_context(tc.psum_pool(name="q_psum", bufs=4))
         logits_psum = ctx.enter_context(tc.psum_pool(name="logits_psum", bufs=2))
 
-        def transpose_rows(rows_sb, n_tiles, pool):
-            words = rows_sb[:].bitcast(F32)
-            banks = []
-            for first in range(0, n_tiles, 2):
-                tiles_here = min(2, n_tiles - first)
-                bank = pool.tile([P, BANK], F32, name="bank")
-                squares = bank[:].rearrange("w (u row) -> w u row", u=2)
-                for r in range(tiles_here):
-                    for u in range(2):
-                        start = (first + r) * WORDS + u * P
-                        nc.tensor.transpose(
-                            out=squares[:, u, r * P : (r + 1) * P],
-                            in_=words[:, start : start + P],
-                            identity=identity[:],
-                        )
-                banks.append((squares, first, tiles_here))
-            return banks
+        def load_rows(rows, name):
+            rows_sb = resident.tile([P, rows.shape[1] * FEATURES], BF16, name=name)
+            nc.sync.dma_start(out=rows_sb[:].rearrange("p (r d) -> p r d", d=FEATURES), in_=rows)
+            return rows_sb
 
-        def regroup(banks, grouped, copies):
-            pairs = grouped[:].bitcast(F32)
-            for (squares, first, tiles_here), copy in zip(banks, copies):
-                copy(
-                    out=pairs[:, first * 2 * P : (first + tiles_here) * 2 * P].rearrange(
-                        "w (row u) -> w row u", u=2
-                    ),
-                    in_=squares[:, :, 0 : tiles_here * P].rearrange("w u row -> w row u"),
-                )
+        def transpose_rows(rows_sb, pool):
+            words = rows_sb[:].bitcast(F32)
+            n_tiles = words.shape[1] // WORDS
+            bank = pool.tile([P, BANK], F32, name="bank")
+            squares = bank[:].rearrange("w (u row) -> w u row", u=2)[:, :, 0 : n_tiles * P]
+            for r in range(n_tiles):
+                for u in range(2):
+                    nc.tensor.transpose(
+                        out=squares[:, u, r * P : (r + 1) * P],
+                        in_=words[:, r * WORDS + u * P : r * WORDS + (u + 1) * P],
+                        identity=identity[:],
+                    )
+            return squares
+
+        def regroup(squares, grouped, first_row, copy):
+            n_rows = squares.shape[2]
+            pairs = grouped[:].bitcast(F32)[:, 2 * first_row : 2 * (first_row + n_rows)]
+            copy(
+                out=pairs.rearrange("w (row u) -> w row u", u=2),
+                in_=squares.rearrange("w u row -> w row u"),
+            )
 
         def quantise(grouped, pool, name):
             n_columns = grouped.shape[1] // PACK
@@ -96,22 +95,24 @@ def tile_actionbindingattention_pb_kernel(tc, slots, ident, Wq, Wk, out):
                 in_=bank[:].rearrange("p (t row) -> p row t", t=PACK),
             )
 
-        def load_rows(rows, n_tiles, pattern, name):
-            rows_sb = resident.tile([P, n_tiles * FEATURES], BF16, name=name)
-            nc.sync.dma_start(
-                out=rows_sb[:].rearrange("p (r d) -> p r d", r=n_tiles),
-                in_=rows.rearrange(pattern, p=P),
-            )
-            return rows_sb
+        def load_weight(weight, name):
+            by_partition = weight.rearrange("(p r) d -> p r d", p=P)
+            return [load_rows(by_partition[:, r : r + 2, :], name + "%d" % r) for r in range(0, PACK, 2)]
 
-        wq_sb = load_rows(Wq, SLAB_TILES, "(p r) d -> p r d", "wq_sb")
-        slots_sb = [load_rows(tokens[0:SLAB, :], SLAB_TILES, "(r p) d -> p r d", "slots_sb0")]
-        wk_sb = load_rows(Wk, SLAB_TILES, "(p r) d -> p r d", "wk_sb")
-        ident_sb = load_rows(ident, 1, "(r p) d -> p r d", "ident_sb")
+        def load_slab(i):
+            return [
+                load_rows(
+                    tokens[first : first + PAIR, :].rearrange("(r p) d -> p r d", p=P), "slots_sb%d" % first
+                )
+                for first in range(i * SLAB, (i + 1) * SLAB, PAIR)
+            ]
+
+        wq_sb = load_weight(Wq, "wq_sb")
+        slots_sb = [load_slab(0)]
+        wk_sb = load_weight(Wk, "wk_sb")
+        ident_sb = load_rows(ident.rearrange("(r p) d -> p r d", p=P), "ident_sb")
         for i in range(1, N_SLABS):
-            slots_sb.append(
-                load_rows(tokens[i * SLAB : (i + 1) * SLAB, :], SLAB_TILES, "(r p) d -> p r d", "slots_sb%d" % i)
-            )
+            slots_sb.append(load_slab(i))
 
         identity = resident.tile([P, P], F32, name="identity")
         masks.make_identity(nc, identity[:])
@@ -119,6 +120,19 @@ def tile_actionbindingattention_pb_kernel(tc, slots, ident, Wq, Wk, out):
         warm = resident.tile([P, 1], F32, name="warm")
         nc.vector.memset(warm[:], 0.0)
         nc.scalar.activation(out=warm[:], in_=warm[:], func=mybir.ActivationFunctionType.Exp)
+
+        word_copies = [nc.vector.tensor_copy, nc.scalar.copy]
+        banks_emptied = []
+
+        def next_word_copy():
+            banks_emptied.append(1)
+            return word_copies[len(banks_emptied) % 2]
+
+        def prepare_weight(weight_sb, name):
+            grouped = resident.tile([P, FEATURES * PACK], BF16, name=name + "_grouped", align_bytes=64)
+            for h, rows_sb in enumerate(weight_sb):
+                regroup(transpose_rows(rows_sb, q_psum), grouped, h * PAIR, next_word_copy())
+            return grouped
 
         slots_banks = {}
         slots_grouped = {}
@@ -131,25 +145,26 @@ def tile_actionbindingattention_pb_kernel(tc, slots, ident, Wq, Wk, out):
         sums = {}
 
         def transpose_slab(i):
-            slots_banks[i] = transpose_rows(slots_sb[i], SLAB_TILES, slots_psum)
+            slots_banks[i] = [transpose_rows(rows_sb, slots_psum) for rows_sb in slots_sb[i]]
 
         def regroup_slab(i):
             slots_grouped[i] = stream.tile([P, SLAB * PACK], BF16, name="slots_grouped", align_bytes=64)
-            regroup(slots_banks[i], slots_grouped[i], [nc.vector.tensor_copy, nc.scalar.copy])
+            for h, squares in enumerate(slots_banks[i]):
+                regroup(squares, slots_grouped[i], h * PAIR, next_word_copy())
 
         def quantise_slab(i):
             slots_mx[i] = quantise(slots_grouped[i], stream, "slots")
 
         def project_slab(i):
             q_grouped[i] = stream.tile([P, SLAB * PACK], BF16, name="q_grouped", align_bytes=64)
-            for row_tile in range(SLAB_TILES):
+            for row_tile in range(SLAB // P):
                 project(wq_mx, slots_mx[i], row_tile, q_grouped[i], nc.any.tensor_copy)
 
         def quantise_q(i):
             q_mx[i] = quantise(q_grouped[i], stream, "q")
 
         def score(i):
-            logits[i] = logits_psum.tile([P, BANK], F32, name="logits")
+            logits[i] = logits_psum.tile([P, SLAB], F32, name="logits")
             nc.tensor.matmul_mx(
                 out=logits[i][:],
                 lhsT=k_mx[0][:].bitcast(FP8X4),
@@ -216,17 +231,15 @@ def tile_actionbindingattention_pb_kernel(tc, slots, ident, Wq, Wk, out):
             if s >= 1:
                 normalise_and_store(s - 1)
 
-        wq_grouped = resident.tile([P, FEATURES * PACK], BF16, name="wq_grouped", align_bytes=64)
-        regroup(transpose_rows(wq_sb, SLAB_TILES, q_psum), wq_grouped, [nc.scalar.copy, nc.scalar.copy])
+        wq_grouped = prepare_weight(wq_sb, "wq")
         transpose_slab(0)
         regroup_slab(0)
         wq_mx = quantise(wq_grouped, resident, "wq")
         quantise_slab(0)
 
-        wk_grouped = resident.tile([P, FEATURES * PACK], BF16, name="wk_grouped", align_bytes=64)
-        regroup(transpose_rows(wk_sb, SLAB_TILES, q_psum), wk_grouped, [nc.scalar.copy, nc.scalar.copy])
+        wk_grouped = prepare_weight(wk_sb, "wk")
         ident_grouped = resident.tile([P, OBJECTS * PACK], BF16, name="ident_grouped", align_bytes=64)
-        regroup(transpose_rows(ident_sb, 1, q_psum), ident_grouped, [nc.scalar.copy])
+        regroup(transpose_rows(ident_sb, q_psum), ident_grouped, 0, next_word_copy())
 
         transpose_slab(1)
         project_slab(0)

@@ -184,7 +184,14 @@ def tile_actionbindingattention_pb_kernel(tc, slots, ident, Wq, Wk, out):
                 op=mybir.AluOpType.max,
             )
             shift[i] = stream.tile([P, SLAB_SAMPLES], F32, name="shift")
-            nc.vector.tensor_scalar_mul(out=shift[i][:], in0=top[:], scalar1=-LOGIT_SCALE)
+            nc.gpsimd.tensor_scalar(
+                out=shift[i][:],
+                in0=top[:],
+                scalar1=-LOGIT_SCALE,
+                scalar2=0.0,
+                op0=mybir.AluOpType.mult,
+                op1=mybir.AluOpType.add,
+            )
 
         def exponentials(i):
             probs[i] = stream.tile([P, SLAB_SAMPLES, SLOTS], F32, name="probs")
@@ -202,7 +209,7 @@ def tile_actionbindingattention_pb_kernel(tc, slots, ident, Wq, Wk, out):
         def normalise_and_store(i):
             inverse = stream.tile([P, SLAB_SAMPLES], F32, name="inverse")
             nc.vector.reciprocal(out=inverse[:], in_=sums[i][:])
-            nc.vector.tensor_tensor(
+            nc.gpsimd.tensor_tensor(
                 out=probs[i][:],
                 in0=probs[i][:],
                 in1=inverse[:].unsqueeze(2).to_broadcast([P, SLAB_SAMPLES, SLOTS]),

from contextlib import ExitStack

import concourse.masks as masks
import concourse.mybir as mybir

F32 = mybir.dt.float32
BF16 = mybir.dt.bfloat16
U32 = mybir.dt.uint32
U8 = mybir.dt.uint8
FP8X4 = mybir.dt.float8_e4m3fn_x4

P = 128
PACK = 4
FEATURES = P * PACK
WORDS = FEATURES // 2
BANK = 512
PAIR = 2 * P

SAMPLES = 64
SLOTS = 64
OBJECTS = 128
SLAB = 256
SLAB_SAMPLES = SLAB // SLOTS
N_SLABS = SAMPLES * SLOTS // SLAB
LOGIT_SCALE = FEATURES**-0.5

FLOPS = 2 * FEATURES * FEATURES * (SAMPLES * SLOTS + OBJECTS) + 2 * SAMPLES * OBJECTS * SLOTS * FEATURES


def tile_actionbindingattention_pb_kernel(tc, slots, ident, Wq, Wk, out):
    nc = tc.nc
    tokens = slots.flatten_outer_dims()

    with ExitStack() as ctx:
        resident = ctx.enter_context(tc.tile_pool(name="resident", bufs=1))
        stream = ctx.enter_context(tc.tile_pool(name="stream", bufs=4))
        slots_psum = ctx.enter_context(tc.psum_pool(name="slots_psum", bufs=2))
        q_psum = ctx.enter_context(tc.psum_pool(name="q_psum", bufs=4))
        logits_psum = ctx.enter_context(tc.psum_pool(name="logits_psum", bufs=2))

        def load_rows(rows, name):
            rows_sb = resident.tile([P, rows.shape[1] * FEATURES], BF16, name=name)
            nc.sync.dma_start(out=rows_sb[:].rearrange("p (r d) -> p r d", d=FEATURES), in_=rows)
            return rows_sb

        def transpose_rows(rows_sb, pool):
            words = rows_sb[:].bitcast(F32)
            n_tiles = words.shape[1] // WORDS
            bank = pool.tile([P, BANK], F32, name="bank")
            squares = bank[:].rearrange("w (u row) -> w u row", u=2)[:, :, 0 : n_tiles * P]
            for r in range(n_tiles):
                for u in range(2):
                    nc.tensor.transpose(
                        out=squares[:, u, r * P : (r + 1) * P],
                        in_=words[:, r * WORDS + u * P : r * WORDS + (u + 1) * P],
                        identity=identity[:],
                    )
            return squares

        def regroup(squares, grouped, first_row, copy):
            n_rows = squares.shape[2]
            pairs = grouped[:].bitcast(F32)[:, 2 * first_row : 2 * (first_row + n_rows)]
            copy(
                out=pairs.rearrange("w (row u) -> w row u", u=2),
                in_=squares.rearrange("w u row -> w row u"),
            )

        def quantise(grouped, pool, name):
            n_columns = grouped.shape[1] // PACK
            codes = pool.tile([P, n_columns], U32, name=name + "_codes", align_bytes=64)
            scales = pool.tile([P, n_columns], U8, name=name + "_scales", align_bytes=64)
            nc.vector.quantize_mx(out=codes[:].bitcast(FP8X4), scales=scales[:], in_=grouped[:])
            return codes, scales

        def project(weights, rows, row_tile, grouped, copy):
            w_codes, w_scales = weights
            r_codes, r_scales = rows
            row_columns = slice(row_tile * P, (row_tile + 1) * P)
            bank = q_psum.tile([P, BANK], F32, name="bank")
            for t in range(PACK):
                feature_columns = slice(t * P, (t + 1) * P)
                nc.tensor.matmul_mx(
                    out=bank[:, feature_columns],
                    lhsT=w_codes[:, feature_columns].bitcast(FP8X4),
                    lhsT_scale=w_scales[:, feature_columns],
                    rhs=r_codes[:, row_columns].bitcast(FP8X4),
                    rhs_scale=r_scales[:, row_columns],
                    start=True,
                    stop=True,
                )
            copy(
                out=grouped[:, row_tile * BANK : (row_tile + 1) * BANK].rearrange(
                    "p (row t) -> p row t", t=PACK
                ),
                in_=bank[:].rearrange("p (t row) -> p row t", t=PACK),
            )

        def load_weight(weight, name):
            by_partition = weight.rearrange("(p r) d -> p r d", p=P)
            return [load_rows(by_partition[:, r : r + 2, :], name + "%d" % r) for r in range(0, PACK, 2)]

        def load_slab(i):
            return [
                load_rows(
                    tokens[first : first + PAIR, :].rearrange("(r p) d -> p r d", p=P), "slots_sb%d" % first
                )
                for first in range(i * SLAB, (i + 1) * SLAB, PAIR)
            ]

        wq_sb = load_weight(Wq, "wq_sb")
        slots_sb = [load_slab(0)]
        wk_sb = load_weight(Wk, "wk_sb")
        ident_sb = load_rows(ident.rearrange("(r p) d -> p r d", p=P), "ident_sb")
        for i in range(1, N_SLABS):
            slots_sb.append(load_slab(i))

        identity = resident.tile([P, P], F32, name="identity")
        masks.make_identity(nc, identity[:])

        warm = resident.tile([P, 1], F32, name="warm")
        nc.vector.memset(warm[:], 0.0)
        nc.scalar.activation(out=warm[:], in_=warm[:], func=mybir.ActivationFunctionType.Exp)

        word_copies = [nc.vector.tensor_copy, nc.scalar.copy]
        banks_emptied = []

        def next_word_copy():
            banks_emptied.append(1)
            return word_copies[len(banks_emptied) % 2]

        def prepare_weight(weight_sb, name):
            grouped = resident.tile([P, FEATURES * PACK], BF16, name=name + "_grouped", align_bytes=64)
            for h, rows_sb in enumerate(weight_sb):
                regroup(transpose_rows(rows_sb, q_psum), grouped, h * PAIR, next_word_copy())
            return grouped

        slots_banks = {}
        slots_grouped = {}
        slots_mx = {}
        q_grouped = {}
        q_mx = {}
        logits = {}
        shift = {}
        probs = {}
        sums = {}

        def transpose_slab(i):
            slots_banks[i] = [transpose_rows(rows_sb, slots_psum) for rows_sb in slots_sb[i]]

        def regroup_slab(i):
            slots_grouped[i] = stream.tile([P, SLAB * PACK], BF16, name="slots_grouped", align_bytes=64)
            for h, squares in enumerate(slots_banks[i]):
                regroup(squares, slots_grouped[i], h * PAIR, next_word_copy())

        def quantise_slab(i):
            slots_mx[i] = quantise(slots_grouped[i], stream, "slots")

        def project_slab(i):
            q_grouped[i] = stream.tile([P, SLAB * PACK], BF16, name="q_grouped", align_bytes=64)
            for row_tile in range(SLAB // P):
                project(wq_mx, slots_mx[i], row_tile, q_grouped[i], nc.any.tensor_copy)

        def quantise_q(i):
            q_mx[i] = quantise(q_grouped[i], stream, "q")

        def score(i):
            logits[i] = logits_psum.tile([P, SLAB], F32, name="logits")
            nc.tensor.matmul_mx(
                out=logits[i][:],
                lhsT=k_mx[0][:].bitcast(FP8X4),
                lhsT_scale=k_mx[1][:],
                rhs=q_mx[i][0][:].bitcast(FP8X4),
                rhs_scale=q_mx[i][1][:],
                start=True,
                stop=True,
            )

        def row_max(i):
            top = stream.tile([P, SLAB_SAMPLES], F32, name="top")
            nc.vector.tensor_reduce(
                out=top[:],
                in_=logits[i][:].rearrange("n (b s) -> n b s", s=SLOTS),
                axis=mybir.AxisListType.X,
                op=mybir.AluOpType.max,
            )
            shift[i] = stream.tile([P, SLAB_SAMPLES], F32, name="shift")
            nc.gpsimd.tensor_scalar(
                out=shift[i][:],
                in0=top[:],
                scalar1=-LOGIT_SCALE,
                scalar2=0.0,
                op0=mybir.AluOpType.mult,
                op1=mybir.AluOpType.add,
            )

        def exponentials(i):
            probs[i] = stream.tile([P, SLAB_SAMPLES, SLOTS], F32, name="probs")
            sums[i] = stream.tile([P, SLAB_SAMPLES], F32, name="sums")
            for b in range(SLAB_SAMPLES):
                nc.scalar.activation(
                    out=probs[i][:, b, :],
                    in_=logits[i][:, b * SLOTS : (b + 1) * SLOTS],
                    func=mybir.ActivationFunctionType.Exp,
                    bias=shift[i][:, b : b + 1],
                    scale=LOGIT_SCALE,
                    accum_out=sums[i][:, b : b + 1],
                )

        def normalise_and_store(i):
            inverse = stream.tile([P, SLAB_SAMPLES], F32, name="inverse")
            nc.vector.reciprocal(out=inverse[:], in_=sums[i][:])
            nc.gpsimd.tensor_tensor(
                out=probs[i][:],
                in0=probs[i][:],
                in1=inverse[:].unsqueeze(2).to_broadcast([P, SLAB_SAMPLES, SLOTS]),
                op=mybir.AluOpType.mult,
            )
            nc.sync.dma_start(
                out=out[i * SLAB_SAMPLES : (i + 1) * SLAB_SAMPLES].rearrange("b n s -> n b s"),
                in_=probs[i][:],
            )

        def pipeline_step(s):
            if s < N_SLABS:
                quantise_q(s)
                score(s)
            if s + 3 < N_SLABS:
                regroup_slab(s + 3)
            if s + 4 < N_SLABS:
                transpose_slab(s + 4)
            if s < N_SLABS:
                row_max(s)
                exponentials(s)
            if s + 2 < N_SLABS:
                project_slab(s + 2)
            if s + 3 < N_SLABS:
                quantise_slab(s + 3)
            if s >= 1:
                normalise_and_store(s - 1)

        wq_grouped = prepare_weight(wq_sb, "wq")
        transpose_slab(0)
        regroup_slab(0)
        wq_mx = quantise(wq_grouped, resident, "wq")
        quantise_slab(0)

        wk_grouped = prepare_weight(wk_sb, "wk")
        ident_grouped = resident.tile([P, OBJECTS * PACK], BF16, name="ident_grouped", align_bytes=64)
        regroup(transpose_rows(ident_sb, q_psum), ident_grouped, 0, next_word_copy())

        transpose_slab(1)
        project_slab(0)
        regroup_slab(1)
        wk_mx = quantise(wk_grouped, resident, "wk")
        ident_mx = quantise(ident_grouped, resident, "ident")
        quantise_slab(1)

        transpose_slab(2)
        regroup_slab(2)
        k_grouped = resident.tile([P, OBJECTS * PACK], BF16, name="k_grouped", align_bytes=64)
        project(wk_mx, ident_mx, 0, k_grouped, nc.scalar.copy)
        project_slab(1)
        k_mx = quantise(k_grouped, resident, "k")
        quantise_slab(2)
        transpose_slab(3)

        for s in range(N_SLABS + 1):
            pipeline_step(s)
